import numpy as np
import ml_dtypes


def mxq(x, axis, fmt="e4m3"):
    dtype, down = {"e4m3": (ml_dtypes.float8_e4m3fn, 7), "e5m2": (ml_dtypes.float8_e5m2, 14)}[fmt]
    v = np.moveaxis(np.asarray(x, np.float32).astype(ml_dtypes.bfloat16).astype(np.float64), axis, -1)
    blocks = v.reshape(v.shape[:-1] + (-1, 32))
    amax = np.abs(blocks).max(-1, keepdims=True)
    byte = np.maximum(np.where(amax > 0, np.frexp(amax)[1] - 1 + 127, 0) - down, 1)
    scale = np.exp2(byte - 127.0)
    codes = (blocks / scale).astype(np.float32).astype(dtype).astype(np.float64)
    return np.moveaxis((codes * scale).reshape(v.shape), -1, axis)


WIDE = False


def mx_kscale(k):
    if not WIDE:
        return np.ones(k)
    levels = np.array([10, -10, 5, -5, 0])
    a = np.random.permutation(np.resize(levels, k // 512 * 4)).reshape(k // 512, 4)
    idx = np.arange(k)
    return np.exp2(a[idx // 512, idx % 128 // 32])


BF16 = ml_dtypes.bfloat16


def bf(x):
    return np.asarray(x, np.float32).astype(BF16)


def f64(x):
    return np.asarray(x).astype(np.float64)


B, CIN, COUT, T, F, KH, KW, PH, PW = 2, 512, 128, 16, 4, 3, 3, 1, 1
OT = T + PH + PH - KH + 1


def setup_inputs():
    s = mx_kscale(CIN)
    return {"x": bf(np.random.standard_normal((B, CIN, T, F)) * s[None, :, None, None]),
            "kernel": bf(np.random.standard_normal((COUT, CIN, F, KH, KW)) / np.sqrt(CIN * KH * KW) / s[None, :, None, None, None]),
            "bias": bf(np.random.standard_normal((1, COUT, 1, F)) * 0.5)}


def reference(x, kernel, bias):
    xq = mxq(f64(x).transpose(3, 2, 0, 1).reshape(F, T * B, CIN), 2, "e4m3")
    kt = f64(kernel).transpose(2, 3, 4, 1, 0)
    out = np.zeros((F, OT * B, COUT))
    for m in range(KH):
        for n in range(KW):
            f0, f1 = max(0, PW - n), min(F, F + PW - n)
            t0, t1 = max(0, PH - m), min(OT, T + PH - m)
            p = xq[f0 + n - PW:f1 + n - PW] @ mxq(kt[f0:f1, m, n], 1, "e4m3")
            p = p[:, (t0 + m - PH) * B:(t1 + m - PH) * B]
            out = out + np.pad(p, ((f0, F - f1), (t0 * B, (OT - t1) * B), (0, 0)))
    return out.reshape(F, OT, B, COUT).transpose(2, 3, 1, 0) + f64(bias)

@@ -1,0 +1,135 @@
+from contextlib import ExitStack
+
+import concourse.mybir as mybir
+
+BF16 = mybir.dt.bfloat16
+F32 = mybir.dt.float32
+U32 = mybir.dt.uint32
+U8 = mybir.dt.uint8
+FP8X4 = mybir.dt.float8_e4m3fn_x4
+
+B, CIN, COUT, T, F, KH, KW = 2, 512, 128, 16, 4, 3, 3
+P = 128
+PACK = 4
+assert CIN == P * PACK
+
+TAPS = F * KH * KW
+O_CHUNK = 16
+N_CHUNKS = COUT // O_CHUNK
+O_HALF = 64
+CHUNKS_PER_HALF = O_HALF // O_CHUNK
+
+FRAMES = B * T
+X_BLOCK = 64
+X_WINDOW = 128
+X_BLOCKS = 16
+
+FLOPS = 2 * CIN * COUT * FRAMES * (TAPS - 2 * KH)
+
+
+def taps_in_f(f):
+    return max(0, 1 - f), min(KW, F + 1 - f)
+
+
+def tile_svconv2d_pa_s_kernel(tc, x, kernel, bias, out):
+    nc = tc.nc
+    with ExitStack() as ctx:
+        keep = ctx.enter_context(tc.tile_pool(name="keep", bufs=1))
+        psum = ctx.enter_context(tc.psum_pool(name="psum", bufs=1))
+
+        x_raw = keep.tile([P, B, PACK, T, F], BF16)
+        nc.scalar.dma_start(
+            out=x_raw[:].rearrange("p b j t f -> p b (j t f)"),
+            in_=x.rearrange("b (p j) t f -> p b (j t f)", j=PACK),
+        )
+        bias_sb = keep.tile([P, F], BF16)
+        nc.scalar.dma_start(out=bias_sb[:], in_=bias[0, :, 0, :])
+
+        kernel_by_channel = kernel.rearrange("o (p j) f m n -> p o (j f m n)", j=PACK)
+        w_raw = []
+        for c in range(N_CHUNKS):
+            raw = keep.tile([P, O_CHUNK * PACK, TAPS], BF16, name="w_raw%d" % c)
+            nc.sync.dma_start(
+                out=raw[:].rearrange("p (o j) s -> p o (j s)", j=PACK),
+                in_=kernel_by_channel[:, c * O_CHUNK : (c + 1) * O_CHUNK, :],
+            )
+            w_raw.append(raw)
+
+        x_shift = keep.tile([P, X_BLOCKS, X_BLOCK // T, T, PACK], BF16, align_bytes=64)
+        nc.vector.memset(x_shift[:], 0.0)
+        for m in range(KH):
+            t_lo, t_hi = max(0, 1 - m), min(T, T + 1 - m)
+            nc.vector.tensor_copy(
+                out=x_shift[:, m * F : (m + 1) * F, 0:B, t_lo:t_hi, :],
+                in_=x_raw[:, :, :, t_lo + m - 1 : t_hi + m - 1, :].rearrange("p b j t f -> p f b t j"),
+            )
+        x_codes = keep.tile([P, X_BLOCKS * X_BLOCK], U32, align_bytes=64)
+        x_scales = keep.tile([P, X_BLOCKS * X_BLOCK], U8, align_bytes=64)
+        nc.vector.quantize_mx(
+            out=x_codes[:].bitcast(FP8X4),
+            scales=x_scales[:],
+            in_=x_shift[:].rearrange("p k c t j -> p (k c t j)"),
+        )
+
+        w_grouped = keep.tile([P, F, KH, KW, COUT * PACK], BF16, align_bytes=64)
+        w_codes = keep.tile([P, F, KH, KW, COUT], U32, align_bytes=64)
+        w_scales = keep.tile([P, F, KH, KW, COUT], U8, align_bytes=64)
+        acc = psum.tile([P, F, X_WINDOW], F32)
+
+        def regroup(c):
+            by_tap = w_raw[c][:].rearrange("p r (f m n) -> p f m r n", f=F, m=KH)
+            rows = slice(c * O_CHUNK * PACK, (c + 1) * O_CHUNK * PACK)
+            for f in range(F):
+                n_lo, n_hi = taps_in_f(f)
+                dst = w_grouped[:, f, :, n_lo:n_hi, rows].rearrange("p m n r -> p m r n")
+                src = by_tap[:, f, :, :, n_lo:n_hi]
+                if f < F // 2:
+                    nc.vector.tensor_copy(out=dst, in_=src)
+                else:
+                    nc.scalar.copy(out=dst, in_=src)
+
+        def quantise(f, m, n, half):
+            cols = slice(half * O_HALF, (half + 1) * O_HALF)
+            nc.vector.quantize_mx(
+                out=w_codes[:, f, m, n, cols].bitcast(FP8X4),
+                scales=w_scales[:, f, m, n, cols],
+                in_=w_grouped[:, f, m, n, half * O_HALF * PACK : (half + 1) * O_HALF * PACK],
+            )
+
+        def multiply(f, m, n):
+            n_lo, n_hi = taps_in_f(f)
+            first = X_BLOCK * (m * F + f + n - 1)
+            window = slice(first, first + X_WINDOW)
+            nc.tensor.matmul_mx(
+                out=acc[:, f, :],
+                lhsT=w_codes[:, f, m, n, :].bitcast(FP8X4),
+                lhsT_scale=w_scales[:, f, m, n, :],
+                rhs=x_codes[:, window].bitcast(FP8X4),
+                rhs_scale=x_scales[:, window],
+                start=(m == 0 and n == n_lo),
+                stop=(m == KH - 1 and n == n_hi - 1),
+            )
+
+        used_taps = [(f, m, n) for f in range(F) for m in range(KH) for n in range(*taps_in_f(f))]
+
+        for c in range(CHUNKS_PER_HALF):
+            regroup(c)
+        for f, m, n in used_taps:
+            quantise(f, m, n, 0)
+        for c in range(CHUNKS_PER_HALF, N_CHUNKS):
+            regroup(c)
+        for f, m, n in used_taps:
+            quantise(f, m, n, 1)
+            multiply(f, m, n)
+
+        result = keep.tile([P, FRAMES, F], F32)
+        nc.vector.tensor_tensor(
+            out=result[:],
+            in0=acc[:, :, 0:FRAMES].rearrange("p f c -> p c f"),
+            in1=bias_sb[:].unsqueeze(1).to_broadcast([P, FRAMES, F]),
+            op=mybir.AluOpType.add,
+        )
+        nc.sync.dma_start(
+            out=out.rearrange("b o t f -> o b (t f)"),
+            in_=result[:].rearrange("p (b t) f -> p b (t f)", b=B),
+        )

@@ -15,9 +15,9 @@ assert CIN == P * PACK
 
 TAPS = F * KH * KW
 O_CHUNK = 16
-N_CHUNKS = COUT // O_CHUNK
+CHUNK_SIZES = [O_CHUNK] * (COUT // O_CHUNK - 1) + [O_CHUNK // 2, O_CHUNK // 4, O_CHUNK // 4]
+CHUNK_STARTS = [sum(CHUNK_SIZES[:c]) for c in range(len(CHUNK_SIZES))]
 O_HALF = 64
-CHUNKS_PER_HALF = O_HALF // O_CHUNK
 
 FRAMES = B * T
 X_BLOCK = 64
@@ -34,6 +34,7 @@ def taps_in_f(f):
 def tile_svconv2d_pa_s_kernel(tc, x, kernel, bias, out):
     nc = tc.nc
     with ExitStack() as ctx:
+        ctx.enter_context(tc.manual_schedule())
         keep = ctx.enter_context(tc.tile_pool(name="keep", bufs=1))
         psum = ctx.enter_context(tc.psum_pool(name="psum", bufs=1))
 
@@ -47,11 +48,11 @@ def tile_svconv2d_pa_s_kernel(tc, x, kernel, bias, out):
 
         kernel_by_channel = kernel.rearrange("o (p j) f m n -> p o (j f m n)", j=PACK)
         w_raw = []
-        for c in range(N_CHUNKS):
-            raw = keep.tile([P, O_CHUNK * PACK, TAPS], BF16, name="w_raw%d" % c)
+        for o_first, o_count in zip(CHUNK_STARTS, CHUNK_SIZES):
+            raw = keep.tile([P, o_count * PACK, TAPS], BF16, name="w_raw%d" % o_first)
             nc.sync.dma_start(
                 out=raw[:].rearrange("p (o j) s -> p o (j s)", j=PACK),
-                in_=kernel_by_channel[:, c * O_CHUNK : (c + 1) * O_CHUNK, :],
+                in_=kernel_by_channel[:, o_first : o_first + o_count, :],
             )
             w_raw.append(raw)
 
@@ -78,7 +79,7 @@ def tile_svconv2d_pa_s_kernel(tc, x, kernel, bias, out):
 
         def regroup(c):
             by_tap = w_raw[c][:].rearrange("p r (f m n) -> p f m r n", f=F, m=KH)
-            rows = slice(c * O_CHUNK * PACK, (c + 1) * O_CHUNK * PACK)
+            rows = slice(CHUNK_STARTS[c] * PACK, (CHUNK_STARTS[c] + CHUNK_SIZES[c]) * PACK)
             for f in range(F):
                 n_lo, n_hi = taps_in_f(f)
                 dst = w_grouped[:, f, :, n_lo:n_hi, rows].rearrange("p m n r -> p m r n")
@@ -112,11 +113,10 @@ def tile_svconv2d_pa_s_kernel(tc, x, kernel, bias, out):
 
         used_taps = [(f, m, n) for f in range(F) for m in range(KH) for n in range(*taps_in_f(f))]
 
-        for c in range(CHUNKS_PER_HALF):
-            regroup(c)
-        for f, m, n in used_taps:
-            quantise(f, m, n, 0)
-        for c in range(CHUNKS_PER_HALF, N_CHUNKS):
+        for c in range(len(CHUNK_SIZES)):
+            if CHUNK_STARTS[c] == O_HALF:
+                for f, m, n in used_taps:
+                    quantise(f, m, n, 0)
             regroup(c)
         for f, m, n in used_taps:
             quantise(f, m, n, 1)

@@ -1,6 +1,7 @@
 from contextlib import ExitStack
 
 import concourse.mybir as mybir
+from concourse.masks import make_identity
 
 BF16 = mybir.dt.bfloat16
 F32 = mybir.dt.float32
@@ -14,10 +15,12 @@ PACK = 4
 assert CIN == P * PACK
 
 TAPS = F * KH * KW
-O_CHUNK = 16
-CHUNK_SIZES = [O_CHUNK] * (COUT // O_CHUNK - 1) + [O_CHUNK // 2, O_CHUNK // 4, O_CHUNK // 4]
-CHUNK_STARTS = [sum(CHUNK_SIZES[:c]) for c in range(len(CHUNK_SIZES))]
-O_HALF = 64
+HALVES = 2
+O_HALF = COUT // HALVES
+I_HALF = CIN // 2
+I_CHUNK = 64
+CHUNKS = I_HALF // I_CHUNK
+BANK_TAPS = 4
 
 FRAMES = B * T
 X_BLOCK = 64
@@ -31,39 +34,49 @@ def taps_in_f(f):
     return max(0, 1 - f), min(KW, F + 1 - f)
 
 
+USED_TAPS = [(f, m, n) for f in range(F) for m in range(KH) for n in range(*taps_in_f(f))]
+BANKS = (len(USED_TAPS) + BANK_TAPS - 1) // BANK_TAPS
+
+
 def tile_svconv2d_pa_s_kernel(tc, x, kernel, bias, out):
     nc = tc.nc
     with ExitStack() as ctx:
-        ctx.enter_context(tc.manual_schedule())
         keep = ctx.enter_context(tc.tile_pool(name="keep", bufs=1))
-        psum = ctx.enter_context(tc.psum_pool(name="psum", bufs=1))
+        turned = ctx.enter_context(tc.psum_pool(name="turned", bufs=7))
+        sums = ctx.enter_context(tc.psum_pool(name="sums", bufs=1))
 
         x_raw = keep.tile([P, B, PACK, T, F], BF16)
-        nc.scalar.dma_start(
-            out=x_raw[:].rearrange("p b j t f -> p b (j t f)"),
-            in_=x.rearrange("b (p j) t f -> p b (j t f)", j=PACK),
-        )
+        for b in range(B):
+            nc.scalar.dma_start(
+                out=x_raw[:, b].rearrange("p (h e) t f -> p h (e t f)", h=2),
+                in_=x[b].rearrange("(h p e) t f -> p h (e t f)", h=2, e=2),
+            )
         bias_sb = keep.tile([P, F], BF16)
         nc.scalar.dma_start(out=bias_sb[:], in_=bias[0, :, 0, :])
 
-        kernel_by_channel = kernel.rearrange("o (p j) f m n -> p o (j f m n)", j=PACK)
-        w_raw = []
-        for o_first, o_count in zip(CHUNK_STARTS, CHUNK_SIZES):
-            raw = keep.tile([P, o_count * PACK, TAPS], BF16, name="w_raw%d" % o_first)
-            nc.sync.dma_start(
-                out=raw[:].rearrange("p (o j) s -> p o (j s)", j=PACK),
-                in_=kernel_by_channel[:, o_first : o_first + o_count, :],
-            )
-            w_raw.append(raw)
+        kernel_rows = kernel.rearrange("(g o) (h i) f m n -> g (o h) (i f m n)", g=HALVES, h=2)
+        w_raw = {}
+        for g in range(HALVES):
+            for c in range(CHUNKS):
+                raw = keep.tile([P, I_CHUNK, TAPS], BF16, name="w_raw%d_%d" % (g, c))
+                nc.sync.dma_start(
+                    out=raw[:].rearrange("p i s -> p (i s)"),
+                    in_=kernel_rows[g, :, c * I_CHUNK * TAPS : (c + 1) * I_CHUNK * TAPS],
+                )
+                w_raw[(g, c)] = raw
+
+        identity = keep.tile([P, P], F32)
+        make_identity(nc, identity[:])
 
         x_shift = keep.tile([P, X_BLOCKS, X_BLOCK // T, T, PACK], BF16, align_bytes=64)
         nc.vector.memset(x_shift[:], 0.0)
         for m in range(KH):
             t_lo, t_hi = max(0, 1 - m), min(T, T + 1 - m)
-            nc.vector.tensor_copy(
-                out=x_shift[:, m * F : (m + 1) * F, 0:B, t_lo:t_hi, :],
-                in_=x_raw[:, :, :, t_lo + m - 1 : t_hi + m - 1, :].rearrange("p b j t f -> p f b t j"),
-            )
+            for b in range(B):
+                nc.scalar.copy(
+                    out=x_shift[:, m * F : (m + 1) * F, b, t_lo:t_hi, :],
+                    in_=x_raw[:, b, :, t_lo + m - 1 : t_hi + m - 1, :].rearrange("p j t f -> p f t j"),
+                )
         x_codes = keep.tile([P, X_BLOCKS * X_BLOCK], U32, align_bytes=64)
         x_scales = keep.tile([P, X_BLOCKS * X_BLOCK], U8, align_bytes=64)
         nc.vector.quantize_mx(
@@ -72,55 +85,76 @@ def tile_svconv2d_pa_s_kernel(tc, x, kernel, bias, out):
             in_=x_shift[:].rearrange("p k c t j -> p (k c t j)"),
         )
 
-        w_grouped = keep.tile([P, F, KH, KW, COUT * PACK], BF16, align_bytes=64)
-        w_codes = keep.tile([P, F, KH, KW, COUT], U32, align_bytes=64)
-        w_scales = keep.tile([P, F, KH, KW, COUT], U8, align_bytes=64)
-        acc = psum.tile([P, F, X_WINDOW], F32)
+        w_taps = [keep.tile([P, F, KH, KW, I_HALF], BF16, name="w_taps%d" % g) for g in range(HALVES)]
+        w_grouped = [
+            keep.tile([P, BANKS * BANK_TAPS, O_HALF * PACK], BF16, name="w_grouped%d" % g, align_bytes=64)
+            for g in range(HALVES)
+        ]
+        w_codes = keep.tile([P, len(USED_TAPS), COUT], U32, align_bytes=64)
+        w_scales = keep.tile([P, len(USED_TAPS), COUT], U8, align_bytes=64)
+        acc = sums.tile([P, F, X_WINDOW], F32)
 
-        def regroup(c):
-            by_tap = w_raw[c][:].rearrange("p r (f m n) -> p f m r n", f=F, m=KH)
-            rows = slice(CHUNK_STARTS[c] * PACK, (CHUNK_STARTS[c] + CHUNK_SIZES[c]) * PACK)
+        def take_apart(g, c):
+            by_tap = w_raw[(g, c)][:].rearrange("p i (f m n) -> p f m i n", f=F, m=KH)
+            channels = slice(c * I_CHUNK, (c + 1) * I_CHUNK)
             for f in range(F):
                 n_lo, n_hi = taps_in_f(f)
-                dst = w_grouped[:, f, :, n_lo:n_hi, rows].rearrange("p m n r -> p m r n")
+                dst = w_taps[g][:, f, :, n_lo:n_hi, channels].rearrange("p m n i -> p m i n")
                 src = by_tap[:, f, :, :, n_lo:n_hi]
-                if f < F // 2:
+                if f < F - 1:
                     nc.vector.tensor_copy(out=dst, in_=src)
                 else:
                     nc.scalar.copy(out=dst, in_=src)
 
-        def quantise(f, m, n, half):
-            cols = slice(half * O_HALF, (half + 1) * O_HALF)
-            nc.vector.quantize_mx(
-                out=w_codes[:, f, m, n, cols].bitcast(FP8X4),
-                scales=w_scales[:, f, m, n, cols],
-                in_=w_grouped[:, f, m, n, half * O_HALF * PACK : (half + 1) * O_HALF * PACK],
+        def turn(g, k):
+            taps = USED_TAPS[k * BANK_TAPS : (k + 1) * BANK_TAPS]
+            bank = turned.tile([P, BANK_TAPS, P], F32)
+            for s, (f, m, n) in enumerate(taps):
+                nc.tensor.transpose(bank[:, s, :], w_taps[g][:, f, m, n, :].bitcast(F32), identity[:])
+            nc.scalar.copy(
+                out=w_grouped[g][:, k * BANK_TAPS : k * BANK_TAPS + len(taps), :].bitcast(F32),
+                in_=bank[:, 0 : len(taps), :],
             )
 
-        def multiply(f, m, n):
-            n_lo, n_hi = taps_in_f(f)
-            first = X_BLOCK * (m * F + f + n - 1)
-            window = slice(first, first + X_WINDOW)
-            nc.tensor.matmul_mx(
-                out=acc[:, f, :],
-                lhsT=w_codes[:, f, m, n, :].bitcast(FP8X4),
-                lhsT_scale=w_scales[:, f, m, n, :],
-                rhs=x_codes[:, window].bitcast(FP8X4),
-                rhs_scale=x_scales[:, window],
-                start=(m == 0 and n == n_lo),
-                stop=(m == KH - 1 and n == n_hi - 1),
-            )
+        def quantise(g, k):
+            cols = slice(g * O_HALF, (g + 1) * O_HALF)
+            for tap in range(k * BANK_TAPS, min((k + 1) * BANK_TAPS, len(USED_TAPS))):
+                nc.vector.quantize_mx(
+                    out=w_codes[:, tap, cols].bitcast(FP8X4),
+                    scales=w_scales[:, tap, cols],
+                    in_=w_grouped[g][:, tap, :],
+                )
 
-        used_taps = [(f, m, n) for f in range(F) for m in range(KH) for n in range(*taps_in_f(f))]
+        def multiply(k):
+            for tap in range(k * BANK_TAPS, min((k + 1) * BANK_TAPS, len(USED_TAPS))):
+                f, m, n = USED_TAPS[tap]
+                n_lo, n_hi = taps_in_f(f)
+                first = X_BLOCK * (m * F + f + n - 1)
+                window = slice(first, first + X_WINDOW)
+                nc.tensor.matmul_mx(
+                    out=acc[:, f, :],
+                    lhsT=w_codes[:, tap, :].bitcast(FP8X4),
+                    lhsT_scale=w_scales[:, tap, :],
+                    rhs=x_codes[:, window].bitcast(FP8X4),
+                    rhs_scale=x_scales[:, window],
+                    start=(m == 0 and n == n_lo),
+                    stop=(m == KH - 1 and n == n_hi - 1),
+                )
 
-        for c in range(len(CHUNK_SIZES)):
-            if CHUNK_STARTS[c] == O_HALF:
-                for f, m, n in used_taps:
-                    quantise(f, m, n, 0)
-            regroup(c)
-        for f, m, n in used_taps:
-            quantise(f, m, n, 1)
-            multiply(f, m, n)
+        for c in range(CHUNKS):
+            take_apart(0, c)
+        banks_per_chunk = BANKS // CHUNKS
+        for c in range(CHUNKS):
+            for k in range(c * banks_per_chunk, (c + 1) * banks_per_chunk):
+                turn(0, k)
+            take_apart(1, c)
+            for k in range(c * banks_per_chunk, (c + 1) * banks_per_chunk):
+                quantise(0, k)
+        for k in range(BANKS):
+            turn(1, k)
+        for k in range(BANKS):
+            quantise(1, k)
+            multiply(k)
 
         result = keep.tile([P, FRAMES, F], F32)
         nc.vector.tensor_tensor(

@@ -18,7 +18,7 @@ TAPS = F * KH * KW
 HALVES = 2
 O_HALF = COUT // HALVES
 I_HALF = CIN // 2
-I_CHUNK = 64
+I_CHUNK = 128
 CHUNKS = I_HALF // I_CHUNK
 BANK_TAPS = 4
 

@@ -18,8 +18,9 @@ TAPS = F * KH * KW
 HALVES = 2
 O_HALF = COUT // HALVES
 I_HALF = CIN // 2
-I_CHUNK = 128
-CHUNKS = I_HALF // I_CHUNK
+LOADS = ((32, 32, 64, 128), (128, 64, 32, 32))
+assert all(sum(widths) == I_HALF for widths in LOADS)
+VECTOR_EMPTIES = ((1, 2), (1, 5))
 BANK_TAPS = 4
 
 FRAMES = B * T
@@ -57,11 +58,12 @@ def tile_svconv2d_pa_s_kernel(tc, x, kernel, bias, out):
         kernel_rows = kernel.rearrange("(g o) (h i) f m n -> g (o h) (i f m n)", g=HALVES, h=2)
         w_raw = {}
         for g in range(HALVES):
-            for c in range(CHUNKS):
-                raw = keep.tile([P, I_CHUNK, TAPS], BF16, name="w_raw%d_%d" % (g, c))
+            for c, width in enumerate(LOADS[g]):
+                first = sum(LOADS[g][:c])
+                raw = keep.tile([P, width, TAPS], BF16, name="w_raw%d_%d" % (g, c))
                 nc.sync.dma_start(
                     out=raw[:].rearrange("p i s -> p (i s)"),
-                    in_=kernel_rows[g, :, c * I_CHUNK * TAPS : (c + 1) * I_CHUNK * TAPS],
+                    in_=kernel_rows[g, :, first * TAPS : (first + width) * TAPS],
                 )
                 w_raw[(g, c)] = raw
 
@@ -79,11 +81,6 @@ def tile_svconv2d_pa_s_kernel(tc, x, kernel, bias, out):
                 )
         x_codes = keep.tile([P, X_BLOCKS * X_BLOCK], U32, align_bytes=64)
         x_scales = keep.tile([P, X_BLOCKS * X_BLOCK], U8, align_bytes=64)
-        nc.vector.quantize_mx(
-            out=x_codes[:].bitcast(FP8X4),
-            scales=x_scales[:],
-            in_=x_shift[:].rearrange("p k c t j -> p (k c t j)"),
-        )
 
         w_taps = [keep.tile([P, F, KH, KW, I_HALF], BF16, name="w_taps%d" % g) for g in range(HALVES)]
         w_grouped = [
@@ -96,7 +93,8 @@ def tile_svconv2d_pa_s_kernel(tc, x, kernel, bias, out):
 
         def take_apart(g, c):
             by_tap = w_raw[(g, c)][:].rearrange("p i (f m n) -> p f m i n", f=F, m=KH)
-            channels = slice(c * I_CHUNK, (c + 1) * I_CHUNK)
+            first = sum(LOADS[g][:c])
+            channels = slice(first, first + LOADS[g][c])
             for f in range(F):
                 n_lo, n_hi = taps_in_f(f)
                 dst = w_taps[g][:, f, :, n_lo:n_hi, channels].rearrange("p m n i -> p m i n")
@@ -111,10 +109,11 @@ def tile_svconv2d_pa_s_kernel(tc, x, kernel, bias, out):
             bank = turned.tile([P, BANK_TAPS, P], F32)
             for s, (f, m, n) in enumerate(taps):
                 nc.tensor.transpose(bank[:, s, :], w_taps[g][:, f, m, n, :].bitcast(F32), identity[:])
-            nc.scalar.copy(
-                out=w_grouped[g][:, k * BANK_TAPS : k * BANK_TAPS + len(taps), :].bitcast(F32),
-                in_=bank[:, 0 : len(taps), :],
-            )
+            dst = w_grouped[g][:, k * BANK_TAPS : k * BANK_TAPS + len(taps), :].bitcast(F32)
+            if (g, k) in VECTOR_EMPTIES:
+                nc.vector.tensor_copy(out=dst, in_=bank[:, 0 : len(taps), :])
+            else:
+                nc.scalar.copy(out=dst, in_=bank[:, 0 : len(taps), :])
 
         def quantise(g, k):
             cols = slice(g * O_HALF, (g + 1) * O_HALF)
@@ -141,17 +140,22 @@ def tile_svconv2d_pa_s_kernel(tc, x, kernel, bias, out):
                     stop=(m == KH - 1 and n == n_hi - 1),
                 )
 
-        for c in range(CHUNKS):
+        for c in range(len(LOADS[0])):
             take_apart(0, c)
-        banks_per_chunk = BANKS // CHUNKS
-        for c in range(CHUNKS):
+        banks_per_chunk = BANKS // len(LOADS[1])
+        for c in range(len(LOADS[1])):
             for k in range(c * banks_per_chunk, (c + 1) * banks_per_chunk):
                 turn(0, k)
             take_apart(1, c)
-            for k in range(c * banks_per_chunk, (c + 1) * banks_per_chunk):
-                quantise(0, k)
         for k in range(BANKS):
             turn(1, k)
+        nc.vector.quantize_mx(
+            out=x_codes[:].bitcast(FP8X4),
+            scales=x_scales[:],
+            in_=x_shift[:].rearrange("p k c t j -> p (k c t j)"),
+        )
+        for k in range(BANKS):
+            quantise(0, k)
         for k in range(BANKS):
             quantise(1, k)
             multiply(k)

@@ -95,14 +95,18 @@ def tile_svconv2d_pa_s_kernel(tc, x, kernel, bias, out):
             by_tap = w_raw[(g, c)][:].rearrange("p i (f m n) -> p f m i n", f=F, m=KH)
             first = sum(LOADS[g][:c])
             channels = slice(first, first + LOADS[g][c])
-            for f in range(F):
+            for f in (0, F - 1):
                 n_lo, n_hi = taps_in_f(f)
                 dst = w_taps[g][:, f, :, n_lo:n_hi, channels].rearrange("p m n i -> p m i n")
                 src = by_tap[:, f, :, :, n_lo:n_hi]
-                if f < F - 1:
+                if f == 0:
                     nc.vector.tensor_copy(out=dst, in_=src)
                 else:
                     nc.scalar.copy(out=dst, in_=src)
+            nc.vector.tensor_copy(
+                out=w_taps[g][:, 1 : F - 1, :, :, channels].rearrange("p f m n i -> p (f m) i n"),
+                in_=by_tap[:, 1 : F - 1].rearrange("p f m i n -> p (f m) i n"),
+            )
 
         def turn(g, k):
             taps = USED_TAPS[k * BANK_TAPS : (k + 1) * BANK_TAPS]

from contextlib import ExitStack

import concourse.mybir as mybir
from concourse.masks import make_identity

BF16 = mybir.dt.bfloat16
F32 = mybir.dt.float32
U32 = mybir.dt.uint32
U8 = mybir.dt.uint8
FP8X4 = mybir.dt.float8_e4m3fn_x4

B, CIN, COUT, T, F, KH, KW = 2, 512, 128, 16, 4, 3, 3
P = 128
PACK = 4
assert CIN == P * PACK

TAPS = F * KH * KW
HALVES = 2
O_HALF = COUT // HALVES
I_HALF = CIN // 2
LOADS = ((32, 32, 64, 128), (128, 64, 32, 32))
assert all(sum(widths) == I_HALF for widths in LOADS)
VECTOR_EMPTIES = ((1, 2), (1, 5))
BANK_TAPS = 4

FRAMES = B * T
X_BLOCK = 64
X_WINDOW = 128
X_BLOCKS = 16

FLOPS = 2 * CIN * COUT * FRAMES * (TAPS - 2 * KH)


def taps_in_f(f):
    return max(0, 1 - f), min(KW, F + 1 - f)


USED_TAPS = [(f, m, n) for f in range(F) for m in range(KH) for n in range(*taps_in_f(f))]
BANKS = (len(USED_TAPS) + BANK_TAPS - 1) // BANK_TAPS


def tile_svconv2d_pa_s_kernel(tc, x, kernel, bias, out):
    nc = tc.nc
    with ExitStack() as ctx:
        keep = ctx.enter_context(tc.tile_pool(name="keep", bufs=1))
        turned = ctx.enter_context(tc.psum_pool(name="turned", bufs=7))
        sums = ctx.enter_context(tc.psum_pool(name="sums", bufs=1))

        x_raw = keep.tile([P, B, PACK, T, F], BF16)
        for b in range(B):
            nc.scalar.dma_start(
                out=x_raw[:, b].rearrange("p (h e) t f -> p h (e t f)", h=2),
                in_=x[b].rearrange("(h p e) t f -> p h (e t f)", h=2, e=2),
            )
        bias_sb = keep.tile([P, F], BF16)
        nc.scalar.dma_start(out=bias_sb[:], in_=bias[0, :, 0, :])

        kernel_rows = kernel.rearrange("(g o) (h i) f m n -> g (o h) (i f m n)", g=HALVES, h=2)
        w_raw = {}
        for g in range(HALVES):
            for c, width in enumerate(LOADS[g]):
                first = sum(LOADS[g][:c])
                raw = keep.tile([P, width, TAPS], BF16, name="w_raw%d_%d" % (g, c))
                nc.sync.dma_start(
                    out=raw[:].rearrange("p i s -> p (i s)"),
                    in_=kernel_rows[g, :, first * TAPS : (first + width) * TAPS],
                )
                w_raw[(g, c)] = raw

        identity = keep.tile([P, P], F32)
        make_identity(nc, identity[:])

        x_shift = keep.tile([P, X_BLOCKS, X_BLOCK // T, T, PACK], BF16, align_bytes=64)
        nc.vector.memset(x_shift[:], 0.0)
        for m in range(KH):
            t_lo, t_hi = max(0, 1 - m), min(T, T + 1 - m)
            for b in range(B):
                nc.scalar.copy(
                    out=x_shift[:, m * F : (m + 1) * F, b, t_lo:t_hi, :],
                    in_=x_raw[:, b, :, t_lo + m - 1 : t_hi + m - 1, :].rearrange("p j t f -> p f t j"),
                )
        x_codes = keep.tile([P, X_BLOCKS * X_BLOCK], U32, align_bytes=64)
        x_scales = keep.tile([P, X_BLOCKS * X_BLOCK], U8, align_bytes=64)

        w_taps = [keep.tile([P, F, KH, KW, I_HALF], BF16, name="w_taps%d" % g) for g in range(HALVES)]
        w_grouped = [
            keep.tile([P, BANKS * BANK_TAPS, O_HALF * PACK], BF16, name="w_grouped%d" % g, align_bytes=64)
            for g in range(HALVES)
        ]
        w_codes = keep.tile([P, len(USED_TAPS), COUT], U32, align_bytes=64)
        w_scales = keep.tile([P, len(USED_TAPS), COUT], U8, align_bytes=64)
        acc = sums.tile([P, F, X_WINDOW], F32)

        def take_apart(g, c):
            by_tap = w_raw[(g, c)][:].rearrange("p i (f m n) -> p f m i n", f=F, m=KH)
            first = sum(LOADS[g][:c])
            channels = slice(first, first + LOADS[g][c])
            for f in (0, F - 1):
                n_lo, n_hi = taps_in_f(f)
                dst = w_taps[g][:, f, :, n_lo:n_hi, channels].rearrange("p m n i -> p m i n")
                src = by_tap[:, f, :, :, n_lo:n_hi]
                if f == 0:
                    nc.vector.tensor_copy(out=dst, in_=src)
                else:
                    nc.scalar.copy(out=dst, in_=src)
            nc.vector.tensor_copy(
                out=w_taps[g][:, 1 : F - 1, :, :, channels].rearrange("p f m n i -> p (f m) i n"),
                in_=by_tap[:, 1 : F - 1].rearrange("p f m i n -> p (f m) i n"),
            )

        def turn(g, k):
            taps = USED_TAPS[k * BANK_TAPS : (k + 1) * BANK_TAPS]
            bank = turned.tile([P, BANK_TAPS, P], F32)
            for s, (f, m, n) in enumerate(taps):
                nc.tensor.transpose(bank[:, s, :], w_taps[g][:, f, m, n, :].bitcast(F32), identity[:])
            dst = w_grouped[g][:, k * BANK_TAPS : k * BANK_TAPS + len(taps), :].bitcast(F32)
            if (g, k) in VECTOR_EMPTIES:
                nc.vector.tensor_copy(out=dst, in_=bank[:, 0 : len(taps), :])
            else:
                nc.scalar.copy(out=dst, in_=bank[:, 0 : len(taps), :])

        def quantise(g, k):
            cols = slice(g * O_HALF, (g + 1) * O_HALF)
            for tap in range(k * BANK_TAPS, min((k + 1) * BANK_TAPS, len(USED_TAPS))):
                nc.vector.quantize_mx(
                    out=w_codes[:, tap, cols].bitcast(FP8X4),
                    scales=w_scales[:, tap, cols],
                    in_=w_grouped[g][:, tap, :],
                )

        def multiply(k):
            for tap in range(k * BANK_TAPS, min((k + 1) * BANK_TAPS, len(USED_TAPS))):
                f, m, n = USED_TAPS[tap]
                n_lo, n_hi = taps_in_f(f)
                first = X_BLOCK * (m * F + f + n - 1)
                window = slice(first, first + X_WINDOW)
                nc.tensor.matmul_mx(
                    out=acc[:, f, :],
                    lhsT=w_codes[:, tap, :].bitcast(FP8X4),
                    lhsT_scale=w_scales[:, tap, :],
                    rhs=x_codes[:, window].bitcast(FP8X4),
                    rhs_scale=x_scales[:, window],
                    start=(m == 0 and n == n_lo),
                    stop=(m == KH - 1 and n == n_hi - 1),
                )

        for c in range(len(LOADS[0])):
            take_apart(0, c)
        banks_per_chunk = BANKS // len(LOADS[1])
        for c in range(len(LOADS[1])):
            for k in range(c * banks_per_chunk, (c + 1) * banks_per_chunk):
                turn(0, k)
            take_apart(1, c)
        for k in range(BANKS):
            turn(1, k)
        nc.vector.quantize_mx(
            out=x_codes[:].bitcast(FP8X4),
            scales=x_scales[:],
            in_=x_shift[:].rearrange("p k c t j -> p (k c t j)"),
        )
        for k in range(BANKS):
            quantise(0, k)
        for k in range(BANKS):
            quantise(1, k)
            multiply(k)

        result = keep.tile([P, FRAMES, F], F32)
        nc.vector.tensor_tensor(
            out=result[:],
            in0=acc[:, :, 0:FRAMES].rearrange("p f c -> p c f"),
            in1=bias_sb[:].unsqueeze(1).to_broadcast([P, FRAMES, F]),
            op=mybir.AluOpType.add,
        )
        nc.sync.dma_start(
            out=out.rearrange("b o t f -> o b (t f)"),
            in_=result[:].rearrange("p (b t) f -> p b (t f)", b=B),
        )
